import numpy as np
import ml_dtypes


def mxq(x, axis, fmt="e4m3"):
    dtype, down = {"e4m3": (ml_dtypes.float8_e4m3fn, 7), "e5m2": (ml_dtypes.float8_e5m2, 14)}[fmt]
    v = np.moveaxis(np.asarray(x, np.float32).astype(ml_dtypes.bfloat16).astype(np.float64), axis, -1)
    blocks = v.reshape(v.shape[:-1] + (-1, 32))
    amax = np.abs(blocks).max(-1, keepdims=True)
    byte = np.maximum(np.where(amax > 0, np.frexp(amax)[1] - 1 + 127, 0) - down, 1)
    scale = np.exp2(byte - 127.0)
    codes = (blocks / scale).astype(np.float32).astype(dtype).astype(np.float64)
    return np.moveaxis((codes * scale).reshape(v.shape), -1, axis)


WIDE = False


def mx_kscale(k):
    if not WIDE:
        return np.ones(k)
    levels = np.array([10, -10, 5, -5, 0])
    a = np.random.permutation(np.resize(levels, k // 512 * 4)).reshape(k // 512, 4)
    idx = np.arange(k)
    return np.exp2(a[idx // 512, idx % 128 // 32])


BF16 = ml_dtypes.bfloat16


def bf(x):
    return np.asarray(x, np.float32).astype(BF16)


def f64(x):
    return np.asarray(x).astype(np.float64)


E2M1 = np.array([0.0, 0.5, 1.0, 1.5, 2.0, 3.0, 4.0, 6.0, -0.0, -0.5, -1.0, -1.5, -2.0, -3.0, -4.0, -6.0])


def pack_weight(w, fmt):
    k, n = w.shape
    w = f64(bf(w)).reshape(k // 32, 32, n)
    amax = np.abs(w).max(1)
    if fmt == "e4m3":
        byte = np.frexp(amax)[1] - 1 + 127 - 7
    else:
        mant, ex = np.frexp(amax / 6.0)
        byte = np.where(mant > 0.5, ex, ex - 1) + 127
    byte = np.clip(np.where(amax > 0, byte, 1), 1, 254)
    scaled = (w * np.exp2(127.0 - byte)[:, None, :]).reshape(k, n).astype(np.float32)
    by_word = np.ascontiguousarray(scaled.reshape(k // 512, 128, 4, n).transpose(0, 1, 3, 2))
    if fmt == "e4m3":
        words = by_word.astype(ml_dtypes.float8_e4m3fn).view(np.uint8)
    else:
        c = by_word.astype(ml_dtypes.float4_e2m1fn).view(np.uint8) & 0xF
        words = c[..., 0::2] | (c[..., 1::2] << 4)
    return np.ascontiguousarray(words), np.ascontiguousarray(byte.astype(np.uint8).reshape(k // 512, 16, n))


def unpack_weight(words, scales, fmt):
    g, p, n, _ = words.shape
    if fmt == "e4m3":
        vals = np.ascontiguousarray(words).view(ml_dtypes.float8_e4m3fn).astype(np.float64)
    else:
        nib = np.empty((g, p, n, 4), np.uint8)
        nib[..., 0::2] = words & 0xF
        nib[..., 1::2] = words >> 4
        vals = E2M1[nib]
    vals = vals * np.repeat(np.exp2(scales.astype(np.float64) - 127.0), 8, axis=1)[..., None]
    return vals.transpose(0, 1, 3, 2).reshape(g * 512, n)

def pack4(w):
    words, scales = pack_weight(w, "e2m1")
    return words.reshape(words.shape[0], 128, -1), scales


def unpack4(words, scales):
    return unpack_weight(words.reshape(words.shape[0], 128, -1, 2), scales, "e2m1")


T, B, I, H = 10, 128, 512, 128


def sigmoid(v):
    return 1.0 / (1.0 + np.exp(-v))


def setup_inputs():
    s = mx_kscale(I)
    input_seq = bf(np.random.standard_normal((T, B, I)) * s)
    w = np.random.standard_normal((3 * H, I)) / np.sqrt(I) / s[None, :]
    words, scales = pack4(np.ascontiguousarray(w.T))
    b_ih = bf(np.random.standard_normal(3 * H) * 0.3)
    gh = bf(np.random.standard_normal((B, 3 * H)) * 0.5)
    return {"input_seq": input_seq,
            "W_ih_words": words,
            "W_ih_scales": scales,
            "b_ih": b_ih,
            "gh": gh}


def reference(input_seq, W_ih_words, W_ih_scales, b_ih, gh):
    gi = (mxq(f64(input_seq), 2, "e4m3") @ unpack4(W_ih_words, W_ih_scales)) + f64(b_ih)
    g = f64(gh)
    i_r, i_z, i_n = gi[..., :H], gi[..., H:2 * H], gi[..., 2 * H:]
    h_r, h_z, h_n = g[..., :H], g[..., H:2 * H], g[..., 2 * H:]
    r = sigmoid(i_r + h_r)
    z = sigmoid(i_z + h_z)
    n = np.tanh(i_n + r * h_n)
    h = (1.0 - z) * n
    return np.transpose(h, (1, 0, 2))

@@ -1,0 +1,124 @@
+from contextlib import ExitStack
+
+import concourse.mybir as mybir
+from concourse.masks import make_identity
+
+F32 = mybir.dt.float32
+BF16 = mybir.dt.bfloat16
+I32 = mybir.dt.int32
+U32 = mybir.dt.uint32
+U8 = mybir.dt.uint8
+FP8X4 = mybir.dt.float8_e4m3fn_x4
+FP4X4 = mybir.dt.float4_e2m1fn_x4
+ACT = mybir.ActivationFunctionType
+ALU = mybir.AluOpType
+
+P = 128
+T, B, K, H = 10, 128, 512, 128
+GATES = 3 * H
+PACK = 4
+HALVES = 2
+GROUP = 2
+BANK = 512
+
+FLOPS = 2 * T * B * K * GATES
+
+
+def tile_grucellmodel_pa_s_kernel(tc, input_seq, W_ih_words, W_ih_scales, b_ih, gh, out):
+    nc = tc.nc
+    with ExitStack() as ctx:
+        const = ctx.enter_context(tc.tile_pool(name="const", bufs=1))
+        xin = ctx.enter_context(tc.tile_pool(name="xin", bufs=T // GROUP))
+        stage = ctx.enter_context(tc.tile_pool(name="stage", bufs=4))
+        gates = ctx.enter_context(tc.tile_pool(name="gates", bufs=3))
+        psum_b = ctx.enter_context(tc.psum_pool(name="psum_b", bufs=1))
+        psum_t = ctx.enter_context(tc.psum_pool(name="psum_t", bufs=3))
+        psum_g = ctx.enter_context(tc.psum_pool(name="psum_g", bufs=4))
+
+        bias_rows = const.tile([P, BANK], BF16)
+        ones = const.tile([P, P], BF16)
+        warm = const.tile([P, 1], F32)
+        ident = const.tile([P, P], F32)
+        gh_sb = const.tile([P, GATES], BF16)
+        addend = const.tile([P, GATES], F32)
+        w_words = const.tile([P, 2 * GATES], U8, align_bytes=64)
+        w_scales = const.tile([P, GATES], U8, align_bytes=64)
+
+        nc.vector.memset(bias_rows[:], 0.0)
+        nc.vector.memset(w_scales[:].bitcast(I32), 0)
+        nc.vector.memset(ones[:], 1.0)
+        nc.vector.memset(warm[:], 0.0)
+        make_identity(nc, ident[:])
+
+        x_tiles = []
+
+        def load_x(g):
+            x_sb = xin.tile([P, GROUP, K], BF16, name="x_sb")
+            steps = input_seq[g * GROUP : (g + 1) * GROUP]
+            nc.sync.dma_start(out=x_sb[:], in_=steps.rearrange("t b k -> b t k"))
+            x_tiles.append(x_sb)
+
+        nc.scalar.dma_start(out=bias_rows[0:1, 0:GATES], in_=b_ih.unsqueeze(0))
+        load_x(0)
+        nc.scalar.dma_start(out=gh_sb[:], in_=gh)
+        nc.sync.dma_start(out=w_words[:].bitcast(I32), in_=W_ih_words[0].bitcast(I32))
+        load_x(1)
+        scale_rows = W_ih_scales[0].bitcast(I32)
+        for r in range(4):
+            nc.sync.dma_start(out=w_scales[r:P:32, :].bitcast(I32), in_=scale_rows[r:16:4, :])
+        for g in range(2, T // GROUP):
+            load_x(g)
+
+        nc.scalar.activation(out=warm[:], in_=warm[:], func=ACT.Sigmoid)
+
+        bias_ps = psum_b.tile([P, BANK], F32)
+        nc.tensor.matmul(out=bias_ps[:], lhsT=ones[:], rhs=bias_rows[:], start=True, stop=True)
+        nc.vector.tensor_tensor(
+            out=addend[:, 0 : 2 * H], in0=bias_ps[:, 0 : 2 * H], in1=gh_sb[:, 0 : 2 * H], op=ALU.add
+        )
+        nc.vector.tensor_copy(out=addend[:, 2 * H : GATES], in_=bias_ps[:, 2 * H : GATES])
+        h_n = gh_sb[:, 2 * H : GATES].unsqueeze(1).to_broadcast([P, GROUP, H])
+
+        for g in range(T // GROUP):
+            pre = gates.tile([P, GROUP, GATES], F32)
+            for j in range(GROUP):
+                x_words = x_tiles[g][:, j, :].bitcast(F32)
+                xt = psum_t.tile([P, HALVES, B], F32)
+                for u in range(HALVES):
+                    nc.tensor.transpose(xt[:, u, :], x_words[:, u : K // 2 : HALVES], ident[:])
+                grouped = stage.tile([P, B, PACK], BF16, align_bytes=64)
+                grouped_flat = grouped[:].rearrange("p b t -> p (b t)")
+                nc.scalar.copy(
+                    out=grouped_flat.bitcast(F32).rearrange("p (b u) -> p b u", u=HALVES),
+                    in_=xt[:].rearrange("p u b -> p b u"),
+                )
+                x_codes = stage.tile([P, B], U32, align_bytes=64)
+                x_scales = stage.tile([P, B], U8, align_bytes=64)
+                nc.vector.quantize_mx(out=x_codes[:].bitcast(FP8X4), scales=x_scales[:], in_=grouped_flat)
+
+                gi = psum_g.tile([P, GATES], F32)
+                for lo, hi in ((0, 2 * H), (2 * H, GATES)):
+                    nc.tensor.matmul_mx(
+                        out=gi[:, lo:hi],
+                        lhsT=x_codes[:].bitcast(FP8X4),
+                        lhsT_scale=x_scales[:],
+                        rhs=w_words[:, 2 * lo : 2 * hi].bitcast(FP4X4),
+                        rhs_scale=w_scales[:, lo:hi],
+                        start=True,
+                        stop=True,
+                    )
+                nc.vector.tensor_tensor(out=pre[:, j, :], in0=gi[:], in1=addend[:], op=ALU.add)
+
+            rz = gates.tile([P, GROUP, 2 * H], F32)
+            nc.scalar.activation(out=rz[:], in_=pre[:, :, 0 : 2 * H], func=ACT.Sigmoid)
+            cand = gates.tile([P, GROUP, H], F32)
+            nc.vector.tensor_tensor(out=cand[:], in0=rz[:, :, 0:H], in1=h_n, op=ALU.mult)
+            nc.vector.tensor_tensor(out=cand[:], in0=cand[:], in1=pre[:, :, 2 * H : GATES], op=ALU.add)
+            n_neg = gates.tile([P, GROUP, H], F32)
+            nc.scalar.activation(out=n_neg[:], in_=cand[:], func=ACT.Tanh, scale=-1.0)
+            h_new = gates.tile([P, GROUP, H], F32)
+            nc.vector.scalar_tensor_tensor(
+                out=h_new[:], in0=rz[:, :, H : 2 * H], scalar=1.0, in1=n_neg[:],
+                op0=ALU.subtract, op1=ALU.mult,
+            )
+            nc.sync.dma_start(out=out[:, g * GROUP : (g + 1) * GROUP, :], in_=h_new[:])

@@ -19,6 +19,7 @@ GATES = 3 * H
 PACK = 4
 HALVES = 2
 GROUP = 2
+N_GROUPS = T // GROUP
 BANK = 512
 
 FLOPS = 2 * T * B * K * GATES
@@ -28,12 +29,13 @@ def tile_grucellmodel_pa_s_kernel(tc, input_seq, W_ih_words, W_ih_scales, b_ih, 
     nc = tc.nc
     with ExitStack() as ctx:
         const = ctx.enter_context(tc.tile_pool(name="const", bufs=1))
-        xin = ctx.enter_context(tc.tile_pool(name="xin", bufs=T // GROUP))
+        xin = ctx.enter_context(tc.tile_pool(name="xin", bufs=N_GROUPS))
         stage = ctx.enter_context(tc.tile_pool(name="stage", bufs=4))
-        gates = ctx.enter_context(tc.tile_pool(name="gates", bufs=3))
+        gates = ctx.enter_context(tc.tile_pool(name="gates", bufs=4))
         psum_b = ctx.enter_context(tc.psum_pool(name="psum_b", bufs=1))
         psum_t = ctx.enter_context(tc.psum_pool(name="psum_t", bufs=3))
         psum_g = ctx.enter_context(tc.psum_pool(name="psum_g", bufs=4))
+        ctx.enter_context(tc.manual_schedule())
 
         bias_rows = const.tile([P, BANK], BF16)
         ones = const.tile([P, P], BF16)
@@ -48,58 +50,56 @@ def tile_grucellmodel_pa_s_kernel(tc, input_seq, W_ih_words, W_ih_scales, b_ih, 
         nc.vector.memset(w_scales[:].bitcast(I32), 0)
         nc.vector.memset(ones[:], 1.0)
         nc.vector.memset(warm[:], 0.0)
-        make_identity(nc, ident[:])
 
-        x_tiles = []
+        x_tiles = {}
 
         def load_x(g):
-            x_sb = xin.tile([P, GROUP, K], BF16, name="x_sb")
+            x_tiles[g] = xin.tile([P, GROUP, K], BF16, name="x_sb")
             steps = input_seq[g * GROUP : (g + 1) * GROUP]
-            nc.sync.dma_start(out=x_sb[:], in_=steps.rearrange("t b k -> b t k"))
-            x_tiles.append(x_sb)
+            nc.sync.dma_start(out=x_tiles[g][:], in_=steps.rearrange("t b k -> b t k"))
 
+        nc.gpsimd.dma_start(out=gh_sb[:], in_=gh)
+        make_identity(nc, ident[:])
         nc.scalar.dma_start(out=bias_rows[0:1, 0:GATES], in_=b_ih.unsqueeze(0))
         load_x(0)
-        nc.scalar.dma_start(out=gh_sb[:], in_=gh)
         nc.sync.dma_start(out=w_words[:].bitcast(I32), in_=W_ih_words[0].bitcast(I32))
-        load_x(1)
         scale_rows = W_ih_scales[0].bitcast(I32)
         for r in range(4):
             nc.sync.dma_start(out=w_scales[r:P:32, :].bitcast(I32), in_=scale_rows[r:16:4, :])
-        for g in range(2, T // GROUP):
+        for g in range(1, N_GROUPS):
             load_x(g)
 
         nc.scalar.activation(out=warm[:], in_=warm[:], func=ACT.Sigmoid)
 
         bias_ps = psum_b.tile([P, BANK], F32)
         nc.tensor.matmul(out=bias_ps[:], lhsT=ones[:], rhs=bias_rows[:], start=True, stop=True)
-        nc.vector.tensor_tensor(
-            out=addend[:, 0 : 2 * H], in0=bias_ps[:, 0 : 2 * H], in1=gh_sb[:, 0 : 2 * H], op=ALU.add
-        )
-        nc.vector.tensor_copy(out=addend[:, 2 * H : GATES], in_=bias_ps[:, 2 * H : GATES])
         h_n = gh_sb[:, 2 * H : GATES].unsqueeze(1).to_broadcast([P, GROUP, H])
 
-        for g in range(T // GROUP):
-            pre = gates.tile([P, GROUP, GATES], F32)
+        grouped, gi, pre, rz, n_neg = {}, {}, {}, {}, {}
+
+        def transpose_x(g):
             for j in range(GROUP):
                 x_words = x_tiles[g][:, j, :].bitcast(F32)
                 xt = psum_t.tile([P, HALVES, B], F32)
                 for u in range(HALVES):
                     nc.tensor.transpose(xt[:, u, :], x_words[:, u : K // 2 : HALVES], ident[:])
-                grouped = stage.tile([P, B, PACK], BF16, align_bytes=64)
-                grouped_flat = grouped[:].rearrange("p b t -> p (b t)")
+                grouped[g, j] = stage.tile([P, B * PACK], BF16, align_bytes=64, name="grouped")
                 nc.scalar.copy(
-                    out=grouped_flat.bitcast(F32).rearrange("p (b u) -> p b u", u=HALVES),
+                    out=grouped[g, j][:].bitcast(F32).rearrange("p (b u) -> p b u", u=HALVES),
                     in_=xt[:].rearrange("p u b -> p b u"),
                 )
+
+        def multiply(g):
+            for j in range(GROUP):
                 x_codes = stage.tile([P, B], U32, align_bytes=64)
                 x_scales = stage.tile([P, B], U8, align_bytes=64)
-                nc.vector.quantize_mx(out=x_codes[:].bitcast(FP8X4), scales=x_scales[:], in_=grouped_flat)
-
-                gi = psum_g.tile([P, GATES], F32)
+                nc.vector.quantize_mx(
+                    out=x_codes[:].bitcast(FP8X4), scales=x_scales[:], in_=grouped[g, j][:]
+                )
+                gi[g, j] = psum_g.tile([P, GATES], F32, name="gi")
                 for lo, hi in ((0, 2 * H), (2 * H, GATES)):
                     nc.tensor.matmul_mx(
-                        out=gi[:, lo:hi],
+                        out=gi[g, j][:, lo:hi],
                         lhsT=x_codes[:].bitcast(FP8X4),
                         lhsT_scale=x_scales[:],
                         rhs=w_words[:, 2 * lo : 2 * hi].bitcast(FP4X4),
@@ -107,18 +107,45 @@ def tile_grucellmodel_pa_s_kernel(tc, input_seq, W_ih_words, W_ih_scales, b_ih, 
                         start=True,
                         stop=True,
                     )
-                nc.vector.tensor_tensor(out=pre[:, j, :], in0=gi[:], in1=addend[:], op=ALU.add)
 
-            rz = gates.tile([P, GROUP, 2 * H], F32)
-            nc.scalar.activation(out=rz[:], in_=pre[:, :, 0 : 2 * H], func=ACT.Sigmoid)
+        def reset_and_update_gates(g):
+            if g == 0:
+                nc.vector.tensor_tensor(
+                    out=addend[:, 0 : 2 * H], in0=bias_ps[:, 0 : 2 * H], in1=gh_sb[:, 0 : 2 * H], op=ALU.add
+                )
+                nc.vector.tensor_copy(out=addend[:, 2 * H : GATES], in_=bias_ps[:, 2 * H : GATES])
+            pre[g] = gates.tile([P, GROUP, GATES], F32, name="pre")
+            for j in range(GROUP):
+                nc.vector.tensor_tensor(out=pre[g][:, j, :], in0=gi[g, j][:], in1=addend[:], op=ALU.add)
+            rz[g] = gates.tile([P, GROUP, 2 * H], F32, name="rz")
+            nc.scalar.activation(out=rz[g][:], in_=pre[g][:, :, 0 : 2 * H], func=ACT.Sigmoid)
+
+        def candidate(g):
             cand = gates.tile([P, GROUP, H], F32)
-            nc.vector.tensor_tensor(out=cand[:], in0=rz[:, :, 0:H], in1=h_n, op=ALU.mult)
-            nc.vector.tensor_tensor(out=cand[:], in0=cand[:], in1=pre[:, :, 2 * H : GATES], op=ALU.add)
-            n_neg = gates.tile([P, GROUP, H], F32)
-            nc.scalar.activation(out=n_neg[:], in_=cand[:], func=ACT.Tanh, scale=-1.0)
+            nc.vector.tensor_tensor(out=cand[:], in0=rz[g][:, :, 0:H], in1=h_n, op=ALU.mult)
+            nc.vector.tensor_tensor(out=cand[:], in0=cand[:], in1=pre[g][:, :, 2 * H : GATES], op=ALU.add)
+            n_neg[g] = gates.tile([P, GROUP, H], F32, name="n_neg")
+            nc.scalar.activation(out=n_neg[g][:], in_=cand[:], func=ACT.Tanh, scale=-1.0)
+
+        def new_state(g):
             h_new = gates.tile([P, GROUP, H], F32)
             nc.vector.scalar_tensor_tensor(
-                out=h_new[:], in0=rz[:, :, H : 2 * H], scalar=1.0, in1=n_neg[:],
+                out=h_new[:], in0=rz[g][:, :, H : 2 * H], scalar=1.0, in1=n_neg[g][:],
                 op0=ALU.subtract, op1=ALU.mult,
             )
             nc.sync.dma_start(out=out[:, g * GROUP : (g + 1) * GROUP, :], in_=h_new[:])
+
+        def live(g):
+            return 0 <= g < N_GROUPS
+
+        for rnd in range(N_GROUPS + 4):
+            if live(rnd - 2):
+                reset_and_update_gates(rnd - 2)
+            if live(rnd - 1):
+                multiply(rnd - 1)
+            if live(rnd):
+                transpose_x(rnd)
+            if live(rnd - 3):
+                candidate(rnd - 3)
+            if live(rnd - 4):
+                new_state(rnd - 4)

@@ -31,11 +31,10 @@ def tile_grucellmodel_pa_s_kernel(tc, input_seq, W_ih_words, W_ih_scales, b_ih, 
         const = ctx.enter_context(tc.tile_pool(name="const", bufs=1))
         xin = ctx.enter_context(tc.tile_pool(name="xin", bufs=N_GROUPS))
         stage = ctx.enter_context(tc.tile_pool(name="stage", bufs=4))
-        gates = ctx.enter_context(tc.tile_pool(name="gates", bufs=4))
+        gates = ctx.enter_context(tc.tile_pool(name="gates", bufs=N_GROUPS))
         psum_b = ctx.enter_context(tc.psum_pool(name="psum_b", bufs=1))
         psum_t = ctx.enter_context(tc.psum_pool(name="psum_t", bufs=3))
         psum_g = ctx.enter_context(tc.psum_pool(name="psum_g", bufs=4))
-        ctx.enter_context(tc.manual_schedule())
 
         bias_rows = const.tile([P, BANK], BF16)
         ones = const.tile([P, P], BF16)
@@ -58,7 +57,6 @@ def tile_grucellmodel_pa_s_kernel(tc, input_seq, W_ih_words, W_ih_scales, b_ih, 
             steps = input_seq[g * GROUP : (g + 1) * GROUP]
             nc.sync.dma_start(out=x_tiles[g][:], in_=steps.rearrange("t b k -> b t k"))
 
-        nc.gpsimd.dma_start(out=gh_sb[:], in_=gh)
         make_identity(nc, ident[:])
         nc.scalar.dma_start(out=bias_rows[0:1, 0:GATES], in_=b_ih.unsqueeze(0))
         load_x(0)
@@ -66,7 +64,9 @@ def tile_grucellmodel_pa_s_kernel(tc, input_seq, W_ih_words, W_ih_scales, b_ih, 
         scale_rows = W_ih_scales[0].bitcast(I32)
         for r in range(4):
             nc.sync.dma_start(out=w_scales[r:P:32, :].bitcast(I32), in_=scale_rows[r:16:4, :])
-        for g in range(1, N_GROUPS):
+        load_x(1)
+        nc.sync.dma_start(out=gh_sb[:], in_=gh)
+        for g in range(2, N_GROUPS):
             load_x(g)
 
         nc.scalar.activation(out=warm[:], in_=warm[:], func=ACT.Sigmoid)
@@ -75,7 +75,7 @@ def tile_grucellmodel_pa_s_kernel(tc, input_seq, W_ih_words, W_ih_scales, b_ih, 
         nc.tensor.matmul(out=bias_ps[:], lhsT=ones[:], rhs=bias_rows[:], start=True, stop=True)
         h_n = gh_sb[:, 2 * H : GATES].unsqueeze(1).to_broadcast([P, GROUP, H])
 
-        grouped, gi, pre, rz, n_neg = {}, {}, {}, {}, {}
+        grouped, gi, pre, rz, cand, n_neg = {}, {}, {}, {}, {}, {}
 
         def transpose_x(g):
             for j in range(GROUP):
@@ -120,12 +120,16 @@ def tile_grucellmodel_pa_s_kernel(tc, input_seq, W_ih_words, W_ih_scales, b_ih, 
             rz[g] = gates.tile([P, GROUP, 2 * H], F32, name="rz")
             nc.scalar.activation(out=rz[g][:], in_=pre[g][:, :, 0 : 2 * H], func=ACT.Sigmoid)
 
+        def reset_hidden(g):
+            cand[g] = gates.tile([P, GROUP, H], F32, name="cand")
+            nc.vector.tensor_tensor(out=cand[g][:], in0=rz[g][:, :, 0:H], in1=h_n, op=ALU.mult)
+
         def candidate(g):
-            cand = gates.tile([P, GROUP, H], F32)
-            nc.vector.tensor_tensor(out=cand[:], in0=rz[g][:, :, 0:H], in1=h_n, op=ALU.mult)
-            nc.vector.tensor_tensor(out=cand[:], in0=cand[:], in1=pre[g][:, :, 2 * H : GATES], op=ALU.add)
+            nc.vector.tensor_tensor(
+                out=cand[g][:], in0=cand[g][:], in1=pre[g][:, :, 2 * H : GATES], op=ALU.add
+            )
             n_neg[g] = gates.tile([P, GROUP, H], F32, name="n_neg")
-            nc.scalar.activation(out=n_neg[g][:], in_=cand[:], func=ACT.Tanh, scale=-1.0)
+            nc.scalar.activation(out=n_neg[g][:], in_=cand[g][:], func=ACT.Tanh, scale=-1.0)
 
         def new_state(g):
             h_new = gates.tile([P, GROUP, H], F32)
@@ -135,17 +139,11 @@ def tile_grucellmodel_pa_s_kernel(tc, input_seq, W_ih_words, W_ih_scales, b_ih, 
             )
             nc.sync.dma_start(out=out[:, g * GROUP : (g + 1) * GROUP, :], in_=h_new[:])
 
-        def live(g):
-            return 0 <= g < N_GROUPS
-
-        for rnd in range(N_GROUPS + 4):
-            if live(rnd - 2):
-                reset_and_update_gates(rnd - 2)
-            if live(rnd - 1):
-                multiply(rnd - 1)
-            if live(rnd):
-                transpose_x(rnd)
-            if live(rnd - 3):
-                candidate(rnd - 3)
-            if live(rnd - 4):
-                new_state(rnd - 4)
+        for g in range(N_GROUPS):
+            transpose_x(g)
+            multiply(g)
+            reset_and_update_gates(g)
+        for g in range(N_GROUPS):
+            reset_hidden(g)
+            candidate(g)
+            new_state(g)

@@ -20,6 +20,7 @@ PACK = 4
 HALVES = 2
 GROUP = 2
 N_GROUPS = T // GROUP
+TAIL_LAG = 2
 BANK = 512
 
 FLOPS = 2 * T * B * K * GATES
@@ -139,11 +140,13 @@ def tile_grucellmodel_pa_s_kernel(tc, input_seq, W_ih_words, W_ih_scales, b_ih, 
             )
             nc.sync.dma_start(out=out[:, g * GROUP : (g + 1) * GROUP, :], in_=h_new[:])
 
+        for g in range(N_GROUPS + TAIL_LAG):
+            if g < N_GROUPS:
+                transpose_x(g)
+                multiply(g)
+                reset_and_update_gates(g)
+            if g >= TAIL_LAG:
+                reset_hidden(g - TAIL_LAG)
+                candidate(g - TAIL_LAG)
         for g in range(N_GROUPS):
-            transpose_x(g)
-            multiply(g)
-            reset_and_update_gates(g)
-        for g in range(N_GROUPS):
-            reset_hidden(g)
-            candidate(g)
             new_state(g)

@@ -18,135 +18,179 @@ T, B, K, H = 10, 128, 512, 128
 GATES = 3 * H
 PACK = 4
 HALVES = 2
-GROUP = 2
-N_GROUPS = T // GROUP
-TAIL_LAG = 2
 BANK = 512
 
 FLOPS = 2 * T * B * K * GATES
 
+CHUNKS = (2, 2, 2, 2, 2)
+LOADS = (2, 2, 2, 2, 2)
+
 
 def tile_grucellmodel_pa_s_kernel(tc, input_seq, W_ih_words, W_ih_scales, b_ih, gh, out):
     nc = tc.nc
+    n_chunks = len(CHUNKS)
+    first = [sum(CHUNKS[:c]) for c in range(n_chunks)]
     with ExitStack() as ctx:
         const = ctx.enter_context(tc.tile_pool(name="const", bufs=1))
-        xin = ctx.enter_context(tc.tile_pool(name="xin", bufs=N_GROUPS))
-        stage = ctx.enter_context(tc.tile_pool(name="stage", bufs=4))
-        gates = ctx.enter_context(tc.tile_pool(name="gates", bufs=N_GROUPS))
-        psum_b = ctx.enter_context(tc.psum_pool(name="psum_b", bufs=1))
+        xin = ctx.enter_context(tc.tile_pool(name="xin", bufs=len(LOADS)))
+        stage = ctx.enter_context(tc.tile_pool(name="stage", bufs=n_chunks))
+        gates = ctx.enter_context(tc.tile_pool(name="gates", bufs=n_chunks))
         psum_t = ctx.enter_context(tc.psum_pool(name="psum_t", bufs=3))
-        psum_g = ctx.enter_context(tc.psum_pool(name="psum_g", bufs=4))
+        psum_rz = ctx.enter_context(tc.psum_pool(name="psum_rz", bufs=2))
+        psum_n = ctx.enter_context(tc.psum_pool(name="psum_n", bufs=1))
 
-        bias_rows = const.tile([P, BANK], BF16)
+        bias_rows = const.tile([P, GATES], BF16)
         ones = const.tile([P, P], BF16)
         warm = const.tile([P, 1], F32)
         ident = const.tile([P, P], F32)
+        ident_bf = const.tile([P, P], BF16)
         gh_sb = const.tile([P, GATES], BF16)
-        addend = const.tile([P, GATES], F32)
+        gh_t = const.tile([P, 2 * H], F32)
+        consts = const.tile([P, H + 4], F32)
         w_words = const.tile([P, 2 * GATES], U8, align_bytes=64)
         w_scales = const.tile([P, GATES], U8, align_bytes=64)
 
-        nc.vector.memset(bias_rows[:], 0.0)
         nc.vector.memset(w_scales[:].bitcast(I32), 0)
+        nc.vector.memset(bias_rows[:], 0.0)
         nc.vector.memset(ones[:], 1.0)
         nc.vector.memset(warm[:], 0.0)
 
-        x_tiles = {}
+        x_step = {}
 
-        def load_x(g):
-            x_tiles[g] = xin.tile([P, GROUP, K], BF16, name="x_sb")
-            steps = input_seq[g * GROUP : (g + 1) * GROUP]
-            nc.sync.dma_start(out=x_tiles[g][:], in_=steps.rearrange("t b k -> b t k"))
+        def load_x(i):
+            t0 = sum(LOADS[:i])
+            x_sb = xin.tile([P, LOADS[i], K], BF16, name="x_sb")
+            nc.sync.dma_start(out=x_sb[:], in_=input_seq[t0 : t0 + LOADS[i]].rearrange("t b k -> b t k"))
+            for j in range(LOADS[i]):
+                x_step[t0 + j] = x_sb[:, j, :]
 
         make_identity(nc, ident[:])
-        nc.scalar.dma_start(out=bias_rows[0:1, 0:GATES], in_=b_ih.unsqueeze(0))
+        nc.scalar.dma_start(out=gh_sb[:], in_=gh)
         load_x(0)
         nc.sync.dma_start(out=w_words[:].bitcast(I32), in_=W_ih_words[0].bitcast(I32))
+        load_x(1)
         scale_rows = W_ih_scales[0].bitcast(I32)
         for r in range(4):
             nc.sync.dma_start(out=w_scales[r:P:32, :].bitcast(I32), in_=scale_rows[r:16:4, :])
-        load_x(1)
-        nc.sync.dma_start(out=gh_sb[:], in_=gh)
-        for g in range(2, N_GROUPS):
-            load_x(g)
+        nc.sync.dma_start(out=bias_rows[0:1, :], in_=b_ih.unsqueeze(0))
+        for i in range(2, len(LOADS)):
+            load_x(i)
 
         nc.scalar.activation(out=warm[:], in_=warm[:], func=ACT.Sigmoid)
+        nc.vector.tensor_copy(out=ident_bf[:], in_=ident[:])
 
-        bias_ps = psum_b.tile([P, BANK], F32)
-        nc.tensor.matmul(out=bias_ps[:], lhsT=ones[:], rhs=bias_rows[:], start=True, stop=True)
-        h_n = gh_sb[:, 2 * H : GATES].unsqueeze(1).to_broadcast([P, GROUP, H])
+        gh_rT = gh_t[:, 0:H]
+        gh_nT = gh_t[:, H : 2 * H]
+        add_z = consts[:, 0:H]
+        b_r = consts[:, H : H + 1]
+        b_n = consts[:, H + 2 : H + 3]
 
-        grouped, gi, pre, rz, cand, n_neg = {}, {}, {}, {}, {}, {}
+        def w_gate(g):
+            return w_words[:, 2 * H * g : 2 * H * (g + 1)].bitcast(FP4X4), w_scales[:, H * g : H * (g + 1)]
 
-        def transpose_x(g):
-            for j in range(GROUP):
-                x_words = x_tiles[g][:, j, :].bitcast(F32)
-                xt = psum_t.tile([P, HALVES, B], F32)
+        def transpose_gh():
+            ps = psum_t.tile([P, 2 * H], F32, tag="turn", name="gh_ps")
+            nc.tensor.matmul(out=ps[:, 0:H], lhsT=gh_sb[:, 0:H], rhs=ident_bf[:], start=True, stop=True)
+            nc.tensor.matmul(out=ps[:, H : 2 * H], lhsT=gh_sb[:, 2 * H : 3 * H], rhs=ident_bf[:], start=True, stop=True)
+            nc.vector.tensor_copy(out=gh_t[:], in_=ps[:])
+
+        def make_consts():
+            ps = psum_t.tile([P, H + 4], F32, tag="turn", name="consts_ps")
+            nc.tensor.matmul(out=ps[:, 0:H], lhsT=ident_bf[:], rhs=gh_sb[:, H : 2 * H], start=True, stop=False)
+            nc.tensor.matmul(out=ps[:, 0:H], lhsT=ones[:], rhs=bias_rows[:, H : 2 * H], start=False, stop=True)
+            nc.tensor.matmul(out=ps[:, H : H + 2], lhsT=bias_rows[:, 0:H], rhs=ones[:, 0:2], start=True, stop=True)
+            nc.tensor.matmul(out=ps[:, H + 2 : H + 4], lhsT=bias_rows[:, 2 * H : 3 * H], rhs=ones[:, 0:2], start=True, stop=True)
+            nc.scalar.copy(out=consts[:], in_=ps[:])
+
+        grouped, g_r, g_z, g_n, r_t, zc, n_t = {}, {}, {}, {}, {}, {}, {}
+        n_banks = [psum_n.tile([P, BANK // B, B], F32, name="n_bank%d" % i) for i in range(3)]
+
+        def transpose_x(c):
+            n = CHUNKS[c]
+            xt = psum_t.tile([P, n, HALVES, B], F32, tag="turn", name="xt")
+            for j in range(n):
+                x_words = x_step[first[c] + j].bitcast(F32)
                 for u in range(HALVES):
-                    nc.tensor.transpose(xt[:, u, :], x_words[:, u : K // 2 : HALVES], ident[:])
-                grouped[g, j] = stage.tile([P, B * PACK], BF16, align_bytes=64, name="grouped")
-                nc.scalar.copy(
-                    out=grouped[g, j][:].bitcast(F32).rearrange("p (b u) -> p b u", u=HALVES),
-                    in_=xt[:].rearrange("p u b -> p b u"),
-                )
-
-        def multiply(g):
-            for j in range(GROUP):
-                x_codes = stage.tile([P, B], U32, align_bytes=64)
-                x_scales = stage.tile([P, B], U8, align_bytes=64)
-                nc.vector.quantize_mx(
-                    out=x_codes[:].bitcast(FP8X4), scales=x_scales[:], in_=grouped[g, j][:]
-                )
-                gi[g, j] = psum_g.tile([P, GATES], F32, name="gi")
-                for lo, hi in ((0, 2 * H), (2 * H, GATES)):
-                    nc.tensor.matmul_mx(
-                        out=gi[g, j][:, lo:hi],
-                        lhsT=x_codes[:].bitcast(FP8X4),
-                        lhsT_scale=x_scales[:],
-                        rhs=w_words[:, 2 * lo : 2 * hi].bitcast(FP4X4),
-                        rhs_scale=w_scales[:, lo:hi],
-                        start=True,
-                        stop=True,
-                    )
-
-        def reset_and_update_gates(g):
-            if g == 0:
-                nc.vector.tensor_tensor(
-                    out=addend[:, 0 : 2 * H], in0=bias_ps[:, 0 : 2 * H], in1=gh_sb[:, 0 : 2 * H], op=ALU.add
-                )
-                nc.vector.tensor_copy(out=addend[:, 2 * H : GATES], in_=bias_ps[:, 2 * H : GATES])
-            pre[g] = gates.tile([P, GROUP, GATES], F32, name="pre")
-            for j in range(GROUP):
-                nc.vector.tensor_tensor(out=pre[g][:, j, :], in0=gi[g, j][:], in1=addend[:], op=ALU.add)
-            rz[g] = gates.tile([P, GROUP, 2 * H], F32, name="rz")
-            nc.scalar.activation(out=rz[g][:], in_=pre[g][:, :, 0 : 2 * H], func=ACT.Sigmoid)
-
-        def reset_hidden(g):
-            cand[g] = gates.tile([P, GROUP, H], F32, name="cand")
-            nc.vector.tensor_tensor(out=cand[g][:], in0=rz[g][:, :, 0:H], in1=h_n, op=ALU.mult)
-
-        def candidate(g):
-            nc.vector.tensor_tensor(
-                out=cand[g][:], in0=cand[g][:], in1=pre[g][:, :, 2 * H : GATES], op=ALU.add
+                    nc.tensor.transpose(xt[:, j, u, :], x_words[:, u : K // 2 : HALVES], ident[:])
+            grouped[c] = stage.tile([P, n * B * PACK], BF16, align_bytes=64, name="grouped")
+            nc.scalar.copy(
+                out=grouped[c][:].bitcast(F32).rearrange("p (j b u) -> p j b u", j=n, u=HALVES),
+                in_=xt[:].rearrange("p j u b -> p j b u"),
             )
-            n_neg[g] = gates.tile([P, GROUP, H], F32, name="n_neg")
-            nc.scalar.activation(out=n_neg[g][:], in_=cand[g][:], func=ACT.Tanh, scale=-1.0)
 
-        def new_state(g):
-            h_new = gates.tile([P, GROUP, H], F32)
-            nc.vector.scalar_tensor_tensor(
-                out=h_new[:], in0=rz[g][:, :, H : 2 * H], scalar=1.0, in1=n_neg[g][:],
-                op0=ALU.subtract, op1=ALU.mult,
-            )
-            nc.sync.dma_start(out=out[:, g * GROUP : (g + 1) * GROUP, :], in_=h_new[:])
+        def multiply(c):
+            n = CHUNKS[c]
+            x_codes = stage.tile([P, n * B], U32, align_bytes=64, name="x_codes")
+            x_scales = stage.tile([P, n * B], U8, align_bytes=64, name="x_scales")
+            nc.vector.quantize_mx(out=x_codes[:].bitcast(FP8X4), scales=x_scales[:], in_=grouped[c][:])
+            g_rz = psum_rz.tile([P, 2, n, B], F32, name="g_rz")
+            g_r[c], g_z[c] = g_rz[:, 0, :, :], g_rz[:, 1, :, :]
+            t0 = first[c]
+            g_n[c] = n_banks[t0 // 4][:, t0 % 4 : t0 % 4 + n, :]
+            for dst, g in ((g_r[c], 0), (g_n[c], 2)):
+                w, ws = w_gate(g)
+                nc.tensor.matmul_mx(
+                    out=dst.rearrange("p j b -> p (j b)"),
+                    lhsT=w, lhsT_scale=ws,
+                    rhs=x_codes[:].bitcast(FP8X4), rhs_scale=x_scales[:],
+                    start=True, stop=True,
+                )
+            w, ws = w_gate(1)
+            for j in range(n):
+                nc.tensor.matmul_mx(
+                    out=g_z[c][:, j, :],
+                    lhsT=x_codes[:, j * B : (j + 1) * B].bitcast(FP8X4), lhsT_scale=x_scales[:, j * B : (j + 1) * B],
+                    rhs=w, rhs_scale=ws,
+                    start=True, stop=True,
+                )
 
-        for g in range(N_GROUPS + TAIL_LAG):
-            if g < N_GROUPS:
-                transpose_x(g)
-                multiply(g)
-                reset_and_update_gates(g)
-            if g >= TAIL_LAG:
-                reset_hidden(g - TAIL_LAG)
-                candidate(g - TAIL_LAG)
-        for g in range(N_GROUPS):
-            new_state(g)
+        def over_steps(ap, n):
+            return ap.unsqueeze(1).to_broadcast([P, n, P])
+
+        def reset_gate(c):
+            n = CHUNKS[c]
+            pre_r = gates.tile([P, n, B], F32, name="pre_r")
+            nc.vector.tensor_tensor(out=pre_r[:], in0=g_r[c], in1=over_steps(gh_rT, n), op=ALU.add)
+            r_t[c] = gates.tile([P, n, B], F32, name="r_t")
+            nc.scalar.activation(out=r_t[c][:], in_=pre_r[:], func=ACT.Sigmoid, bias=b_r)
+
+        def update_gate(c):
+            n = CHUNKS[c]
+            pre_z = gates.tile([P, n, H], F32, name="pre_z")
+            nc.vector.tensor_tensor(out=pre_z[:], in0=g_z[c], in1=over_steps(add_z, n), op=ALU.add)
+            zc[c] = gates.tile([P, n, H], F32, name="zc")
+            nc.scalar.activation(out=zc[c][:], in_=pre_z[:], func=ACT.Sigmoid, scale=-1.0)
+
+        def candidate(c):
+            n = CHUNKS[c]
+            cand = gates.tile([P, n, B], F32, name="cand")
+            nc.vector.tensor_tensor(out=cand[:], in0=r_t[c][:], in1=over_steps(gh_nT, n), op=ALU.mult)
+            pre_n = gates.tile([P, n, B], F32, name="pre_n")
+            nc.vector.tensor_tensor(out=pre_n[:], in0=g_n[c], in1=cand[:], op=ALU.add)
+            n_t[c] = gates.tile([P, n, B], F32, name="n_t")
+            nc.scalar.activation(out=n_t[c][:], in_=pre_n[:], func=ACT.Tanh, bias=b_n)
+
+        def new_state(c):
+            n = CHUNKS[c]
+            n_ps = psum_t.tile([P, n, H], F32, tag="turn", name="n_ps")
+            for j in range(n):
+                nc.tensor.transpose(n_ps[:, j, :], n_t[c][:, j, :], ident[:])
+            h_new = gates.tile([P, n, H], F32, name="h_new")
+            nc.vector.tensor_tensor(out=h_new[:], in0=n_ps[:], in1=zc[c][:], op=ALU.mult)
+            nc.sync.dma_start(out=out[:, first[c] : first[c] + n, :], in_=h_new[:])
+
+        def front(c):
+            transpose_x(c)
+            if c == 0:
+                transpose_gh()
+
+        def middle(c):
+            multiply(c)
+            if c == 0:
+                make_consts()
+
+        stages = ((front, 0), (middle, 1), (reset_gate, 2), (update_gate, 3), (candidate, 2), (new_state, 6))
+        for tick in range(n_chunks + 6):
+            for work, lag in stages:
+                if 0 <= tick - lag < n_chunks:
+                    work(tick - lag)

@@ -164,7 +164,7 @@ def tile_grucellmodel_pa_s_kernel(tc, input_seq, W_ih_words, W_ih_scales, b_ih, 
         def candidate(c):
             n = CHUNKS[c]
             cand = gates.tile([P, n, B], F32, name="cand")
-            nc.vector.tensor_tensor(out=cand[:], in0=r_t[c][:], in1=over_steps(gh_nT, n), op=ALU.mult)
+            nc.gpsimd.tensor_tensor(out=cand[:], in0=r_t[c][:], in1=over_steps(gh_nT, n), op=ALU.mult)
             pre_n = gates.tile([P, n, B], F32, name="pre_n")
             nc.vector.tensor_tensor(out=pre_n[:], in0=g_n[c], in1=cand[:], op=ALU.add)
             n_t[c] = gates.tile([P, n, B], F32, name="n_t")

@@ -22,8 +22,7 @@ BANK = 512
 
 FLOPS = 2 * T * B * K * GATES
 
-CHUNKS = (2, 2, 2, 2, 2)
-LOADS = (2, 2, 2, 2, 2)
+CHUNKS = (1, 2, 2, 2, 2, 1)
 
 
 def tile_grucellmodel_pa_s_kernel(tc, input_seq, W_ih_words, W_ih_scales, b_ih, gh, out):
@@ -32,7 +31,7 @@ def tile_grucellmodel_pa_s_kernel(tc, input_seq, W_ih_words, W_ih_scales, b_ih, 
     first = [sum(CHUNKS[:c]) for c in range(n_chunks)]
     with ExitStack() as ctx:
         const = ctx.enter_context(tc.tile_pool(name="const", bufs=1))
-        xin = ctx.enter_context(tc.tile_pool(name="xin", bufs=len(LOADS)))
+        xin = ctx.enter_context(tc.tile_pool(name="xin", bufs=n_chunks))
         stage = ctx.enter_context(tc.tile_pool(name="stage", bufs=n_chunks))
         gates = ctx.enter_context(tc.tile_pool(name="gates", bufs=n_chunks))
         psum_t = ctx.enter_context(tc.psum_pool(name="psum_t", bufs=3))
@@ -55,26 +54,25 @@ def tile_grucellmodel_pa_s_kernel(tc, input_seq, W_ih_words, W_ih_scales, b_ih, 
         nc.vector.memset(ones[:], 1.0)
         nc.vector.memset(warm[:], 0.0)
 
-        x_step = {}
+        x_tiles = {}
 
-        def load_x(i):
-            t0 = sum(LOADS[:i])
-            x_sb = xin.tile([P, LOADS[i], K], BF16, name="x_sb")
-            nc.sync.dma_start(out=x_sb[:], in_=input_seq[t0 : t0 + LOADS[i]].rearrange("t b k -> b t k"))
-            for j in range(LOADS[i]):
-                x_step[t0 + j] = x_sb[:, j, :]
+        def load_x(c):
+            x_tiles[c] = xin.tile([P, CHUNKS[c], K], BF16, name="x_sb")
+            steps = input_seq[first[c] : first[c] + CHUNKS[c]]
+            nc.sync.dma_start(out=x_tiles[c][:], in_=steps.rearrange("t b k -> b t k"))
 
         make_identity(nc, ident[:])
         nc.scalar.dma_start(out=gh_sb[:], in_=gh)
         load_x(0)
         nc.sync.dma_start(out=w_words[:].bitcast(I32), in_=W_ih_words[0].bitcast(I32))
-        load_x(1)
         scale_rows = W_ih_scales[0].bitcast(I32)
         for r in range(4):
             nc.sync.dma_start(out=w_scales[r:P:32, :].bitcast(I32), in_=scale_rows[r:16:4, :])
+        load_x(1)
+        load_x(2)
         nc.sync.dma_start(out=bias_rows[0:1, :], in_=b_ih.unsqueeze(0))
-        for i in range(2, len(LOADS)):
-            load_x(i)
+        for c in range(3, n_chunks):
+            load_x(c)
 
         nc.scalar.activation(out=warm[:], in_=warm[:], func=ACT.Sigmoid)
         nc.vector.tensor_copy(out=ident_bf[:], in_=ident[:])
@@ -102,32 +100,49 @@ def tile_grucellmodel_pa_s_kernel(tc, input_seq, W_ih_words, W_ih_scales, b_ih, 
             nc.tensor.matmul(out=ps[:, H + 2 : H + 4], lhsT=bias_rows[:, 2 * H : 3 * H], rhs=ones[:, 0:2], start=True, stop=True)
             nc.scalar.copy(out=consts[:], in_=ps[:])
 
-        grouped, g_r, g_z, g_n, r_t, zc, n_t = {}, {}, {}, {}, {}, {}, {}
+        t = {}
         n_banks = [psum_n.tile([P, BANK // B, B], F32, name="n_bank%d" % i) for i in range(3)]
+        n_place = []
+        for n in CHUNKS:
+            bank, slot = n_place[-1] if n_place else (0, 0)
+            slot += CHUNKS[len(n_place) - 1] if n_place else 0
+            if slot + n > BANK // B:
+                bank, slot = bank + 1, 0
+            n_place.append((bank, slot))
 
-        def transpose_x(c):
+        def over_steps(ap, n):
+            return ap.unsqueeze(1).to_broadcast([P, n, P])
+
+        def turn_x(c):
             n = CHUNKS[c]
-            xt = psum_t.tile([P, n, HALVES, B], F32, tag="turn", name="xt")
+            t["xt", c] = psum_t.tile([P, n, HALVES, B], F32, tag="turn", name="xt")
             for j in range(n):
-                x_words = x_step[first[c] + j].bitcast(F32)
+                x_words = x_tiles[c][:, j, :].bitcast(F32)
                 for u in range(HALVES):
-                    nc.tensor.transpose(xt[:, j, u, :], x_words[:, u : K // 2 : HALVES], ident[:])
-            grouped[c] = stage.tile([P, n * B * PACK], BF16, align_bytes=64, name="grouped")
+                    nc.tensor.transpose(t["xt", c][:, j, u, :], x_words[:, u : K // 2 : HALVES], ident[:])
+
+        def group_x(c):
+            n = CHUNKS[c]
+            t["grouped", c] = stage.tile([P, n * B * PACK], BF16, align_bytes=64, name="grouped")
             nc.scalar.copy(
-                out=grouped[c][:].bitcast(F32).rearrange("p (j b u) -> p j b u", j=n, u=HALVES),
-                in_=xt[:].rearrange("p j u b -> p j b u"),
+                out=t["grouped", c][:].bitcast(F32).rearrange("p (j b u) -> p j b u", j=n, u=HALVES),
+                in_=t["xt", c][:].rearrange("p j u b -> p j b u"),
             )
+
+        def quantise_x(c):
+            n = CHUNKS[c]
+            t["codes", c] = stage.tile([P, n * B], U32, align_bytes=64, name="x_codes")
+            t["scales", c] = stage.tile([P, n * B], U8, align_bytes=64, name="x_scales")
+            nc.vector.quantize_mx(out=t["codes", c][:].bitcast(FP8X4), scales=t["scales", c][:], in_=t["grouped", c][:])
 
         def multiply(c):
             n = CHUNKS[c]
-            x_codes = stage.tile([P, n * B], U32, align_bytes=64, name="x_codes")
-            x_scales = stage.tile([P, n * B], U8, align_bytes=64, name="x_scales")
-            nc.vector.quantize_mx(out=x_codes[:].bitcast(FP8X4), scales=x_scales[:], in_=grouped[c][:])
+            x_codes, x_scales = t["codes", c], t["scales", c]
             g_rz = psum_rz.tile([P, 2, n, B], F32, name="g_rz")
-            g_r[c], g_z[c] = g_rz[:, 0, :, :], g_rz[:, 1, :, :]
-            t0 = first[c]
-            g_n[c] = n_banks[t0 // 4][:, t0 % 4 : t0 % 4 + n, :]
-            for dst, g in ((g_r[c], 0), (g_n[c], 2)):
+            t["g_r", c], t["g_z", c] = g_rz[:, 0, :, :], g_rz[:, 1, :, :]
+            bank, slot = n_place[c]
+            t["g_n", c] = n_banks[bank][:, slot : slot + n, :]
+            for dst, g in ((t["g_r", c], 0), (t["g_n", c], 2)):
                 w, ws = w_gate(g)
                 nc.tensor.matmul_mx(
                     out=dst.rearrange("p j b -> p (j b)"),
@@ -138,59 +153,65 @@ def tile_grucellmodel_pa_s_kernel(tc, input_seq, W_ih_words, W_ih_scales, b_ih, 
             w, ws = w_gate(1)
             for j in range(n):
                 nc.tensor.matmul_mx(
-                    out=g_z[c][:, j, :],
+                    out=t["g_z", c][:, j, :],
                     lhsT=x_codes[:, j * B : (j + 1) * B].bitcast(FP8X4), lhsT_scale=x_scales[:, j * B : (j + 1) * B],
                     rhs=w, rhs_scale=ws,
                     start=True, stop=True,
                 )
 
-        def over_steps(ap, n):
-            return ap.unsqueeze(1).to_broadcast([P, n, P])
-
-        def reset_gate(c):
+        def add_r(c):
             n = CHUNKS[c]
-            pre_r = gates.tile([P, n, B], F32, name="pre_r")
-            nc.vector.tensor_tensor(out=pre_r[:], in0=g_r[c], in1=over_steps(gh_rT, n), op=ALU.add)
-            r_t[c] = gates.tile([P, n, B], F32, name="r_t")
-            nc.scalar.activation(out=r_t[c][:], in_=pre_r[:], func=ACT.Sigmoid, bias=b_r)
+            t["pre_r", c] = gates.tile([P, n, B], F32, name="pre_r")
+            nc.vector.tensor_tensor(out=t["pre_r", c][:], in0=t["g_r", c], in1=over_steps(gh_rT, n), op=ALU.add)
 
-        def update_gate(c):
-            n = CHUNKS[c]
-            pre_z = gates.tile([P, n, H], F32, name="pre_z")
-            nc.vector.tensor_tensor(out=pre_z[:], in0=g_z[c], in1=over_steps(add_z, n), op=ALU.add)
-            zc[c] = gates.tile([P, n, H], F32, name="zc")
-            nc.scalar.activation(out=zc[c][:], in_=pre_z[:], func=ACT.Sigmoid, scale=-1.0)
+        def sigmoid_r(c):
+            t["r", c] = gates.tile([P, CHUNKS[c], B], F32, name="r_t")
+            nc.scalar.activation(out=t["r", c][:], in_=t["pre_r", c][:], func=ACT.Sigmoid, bias=b_r)
 
-        def candidate(c):
+        def add_z_gate(c):
             n = CHUNKS[c]
-            cand = gates.tile([P, n, B], F32, name="cand")
-            nc.gpsimd.tensor_tensor(out=cand[:], in0=r_t[c][:], in1=over_steps(gh_nT, n), op=ALU.mult)
-            pre_n = gates.tile([P, n, B], F32, name="pre_n")
-            nc.vector.tensor_tensor(out=pre_n[:], in0=g_n[c], in1=cand[:], op=ALU.add)
-            n_t[c] = gates.tile([P, n, B], F32, name="n_t")
-            nc.scalar.activation(out=n_t[c][:], in_=pre_n[:], func=ACT.Tanh, bias=b_n)
+            t["pre_z", c] = gates.tile([P, n, H], F32, name="pre_z")
+            nc.vector.tensor_tensor(out=t["pre_z", c][:], in0=t["g_z", c], in1=over_steps(add_z, n), op=ALU.add)
+
+        def sigmoid_z(c):
+            t["zc", c] = gates.tile([P, CHUNKS[c], H], F32, name="zc")
+            nc.scalar.activation(out=t["zc", c][:], in_=t["pre_z", c][:], func=ACT.Sigmoid, scale=-1.0)
+
+        def reset_hidden(c):
+            n = CHUNKS[c]
+            t["cand", c] = gates.tile([P, n, B], F32, name="cand")
+            nc.gpsimd.tensor_tensor(out=t["cand", c][:], in0=t["r", c][:], in1=over_steps(gh_nT, n), op=ALU.mult)
+
+        def add_n(c):
+            t["pre_n", c] = gates.tile([P, CHUNKS[c], B], F32, name="pre_n")
+            nc.vector.tensor_tensor(out=t["pre_n", c][:], in0=t["g_n", c], in1=t["cand", c][:], op=ALU.add)
+
+        def tanh_n(c):
+            t["n", c] = gates.tile([P, CHUNKS[c], B], F32, name="n_t")
+            nc.scalar.activation(out=t["n", c][:], in_=t["pre_n", c][:], func=ACT.Tanh, bias=b_n)
+
+        def turn_n(c):
+            n = CHUNKS[c]
+            t["n_ps", c] = psum_t.tile([P, n, H], F32, tag="turn", name="n_ps")
+            for j in range(n):
+                nc.tensor.transpose(t["n_ps", c][:, j, :], t["n", c][:, j, :], ident[:])
 
         def new_state(c):
             n = CHUNKS[c]
-            n_ps = psum_t.tile([P, n, H], F32, tag="turn", name="n_ps")
-            for j in range(n):
-                nc.tensor.transpose(n_ps[:, j, :], n_t[c][:, j, :], ident[:])
             h_new = gates.tile([P, n, H], F32, name="h_new")
-            nc.vector.tensor_tensor(out=h_new[:], in0=n_ps[:], in1=zc[c][:], op=ALU.mult)
+            nc.vector.tensor_tensor(out=h_new[:], in0=t["n_ps", c][:], in1=t["zc", c][:], op=ALU.mult)
             nc.sync.dma_start(out=out[:, first[c] : first[c] + n, :], in_=h_new[:])
 
-        def front(c):
-            transpose_x(c)
-            if c == 0:
+        chain = (
+            (turn_x, 0), (group_x, 1), (quantise_x, 2), (multiply, 3), (add_r, 4), (sigmoid_r, 5), (add_z_gate, 5),
+            (sigmoid_z, 6), (reset_hidden, 6), (add_n, 7), (tanh_n, 8), (turn_n, 9), (new_state, 10),
+        )
+        ctx.enter_context(tc.manual_schedule())
+        for rnd in range(n_chunks + 10):
+            for work, lag in reversed(chain):
+                if 0 <= rnd - lag < n_chunks:
+                    work(rnd - lag)
+            if rnd == 1:
                 transpose_gh()
-
-        def middle(c):
-            multiply(c)
-            if c == 0:
+            if rnd == 3:
                 make_consts()
-
-        stages = ((front, 0), (middle, 1), (reset_gate, 2), (update_gate, 3), (candidate, 2), (new_state, 6))
-        for tick in range(n_chunks + 6):
-            for work, lag in stages:
-                if 0 <= tick - lag < n_chunks:
-                    work(tick - lag)

@@ -207,6 +207,9 @@ def tile_grucellmodel_pa_s_kernel(tc, input_seq, W_ih_words, W_ih_scales, b_ih, 
             (sigmoid_z, 6), (reset_hidden, 6), (add_n, 7), (tanh_n, 8), (turn_n, 9), (new_state, 10),
         )
         ctx.enter_context(tc.manual_schedule())
+        warm_ps = psum_t.tile([P, BANK // P, P], F32, tag="turn", name="warm_ps")
+        for j in range(8):
+            nc.tensor.transpose(warm_ps[:, j % (BANK // P), :], ident[:], ident[:])
         for rnd in range(n_chunks + 10):
             for work, lag in reversed(chain):
                 if 0 <= rnd - lag < n_chunks:

@@ -64,12 +64,12 @@ def tile_grucellmodel_pa_s_kernel(tc, input_seq, W_ih_words, W_ih_scales, b_ih, 
         make_identity(nc, ident[:])
         nc.scalar.dma_start(out=gh_sb[:], in_=gh)
         load_x(0)
+        load_x(1)
+        load_x(2)
         nc.sync.dma_start(out=w_words[:].bitcast(I32), in_=W_ih_words[0].bitcast(I32))
         scale_rows = W_ih_scales[0].bitcast(I32)
         for r in range(4):
             nc.sync.dma_start(out=w_scales[r:P:32, :].bitcast(I32), in_=scale_rows[r:16:4, :])
-        load_x(1)
-        load_x(2)
         nc.sync.dma_start(out=bias_rows[0:1, :], in_=b_ih.unsqueeze(0))
         for c in range(3, n_chunks):
             load_x(c)
@@ -214,7 +214,7 @@ def tile_grucellmodel_pa_s_kernel(tc, input_seq, W_ih_words, W_ih_scales, b_ih, 
             for work, lag in reversed(chain):
                 if 0 <= rnd - lag < n_chunks:
                     work(rnd - lag)
-            if rnd == 1:
+            if rnd == 0:
                 transpose_gh()
-            if rnd == 3:
+            if rnd == 2:
                 make_consts()

@@ -49,8 +49,8 @@ def tile_grucellmodel_pa_s_kernel(tc, input_seq, W_ih_words, W_ih_scales, b_ih, 
         w_words = const.tile([P, 2 * GATES], U8, align_bytes=64)
         w_scales = const.tile([P, GATES], U8, align_bytes=64)
 
-        nc.vector.memset(w_scales[:].bitcast(I32), 0)
         nc.vector.memset(bias_rows[:], 0.0)
+        nc.vector.memset(w_scales[:].bitcast(I32), 0)
         nc.vector.memset(ones[:], 1.0)
         nc.vector.memset(warm[:], 0.0)
 
@@ -64,14 +64,15 @@ def tile_grucellmodel_pa_s_kernel(tc, input_seq, W_ih_words, W_ih_scales, b_ih, 
         make_identity(nc, ident[:])
         nc.scalar.dma_start(out=gh_sb[:], in_=gh)
         load_x(0)
+        nc.sync.dma_start(out=bias_rows[0:1, :], in_=b_ih.unsqueeze(0))
         load_x(1)
         load_x(2)
         nc.sync.dma_start(out=w_words[:].bitcast(I32), in_=W_ih_words[0].bitcast(I32))
+        load_x(3)
         scale_rows = W_ih_scales[0].bitcast(I32)
         for r in range(4):
             nc.sync.dma_start(out=w_scales[r:P:32, :].bitcast(I32), in_=scale_rows[r:16:4, :])
-        nc.sync.dma_start(out=bias_rows[0:1, :], in_=b_ih.unsqueeze(0))
-        for c in range(3, n_chunks):
+        for c in range(4, n_chunks):
             load_x(c)
 
         nc.scalar.activation(out=warm[:], in_=warm[:], func=ACT.Sigmoid)

@@ -204,16 +204,18 @@ def tile_grucellmodel_pa_s_kernel(tc, input_seq, W_ih_words, W_ih_scales, b_ih, 
             nc.sync.dma_start(out=out[:, first[c] : first[c] + n, :], in_=h_new[:])
 
         chain = (
-            (turn_x, 0), (group_x, 1), (quantise_x, 2), (multiply, 3), (add_r, 4), (sigmoid_r, 5), (add_z_gate, 5),
-            (sigmoid_z, 6), (reset_hidden, 6), (add_n, 7), (tanh_n, 8), (turn_n, 9), (new_state, 10),
+            (turn_x, 0), (group_x, 1), (quantise_x, 2), (multiply, 3), (add_z_gate, 4), (add_r, 4), (sigmoid_z, 5),
+            (sigmoid_r, 5), (reset_hidden, 6), (add_n, 7), (tanh_n, 8), (turn_n, 9), (new_state, 10),
         )
         ctx.enter_context(tc.manual_schedule())
         warm_ps = psum_t.tile([P, BANK // P, P], F32, tag="turn", name="warm_ps")
         for j in range(8):
             nc.tensor.transpose(warm_ps[:, j % (BANK // P), :], ident[:], ident[:])
         for rnd in range(n_chunks + 10):
+            if rnd == 3:
+                turn_x(rnd)
             for work, lag in reversed(chain):
-                if 0 <= rnd - lag < n_chunks:
+                if 0 <= rnd - lag < n_chunks and not (rnd == 3 and lag == 0):
                     work(rnd - lag)
             if rnd == 0:
                 transpose_gh()

@@ -23,6 +23,7 @@ BANK = 512
 FLOPS = 2 * T * B * K * GATES
 
 CHUNKS = (1, 2, 2, 2, 2, 1)
+Z_GROUPS = ((0,), (1, 2), (3, 4, 5))
 
 
 def tile_grucellmodel_pa_s_kernel(tc, input_seq, W_ih_words, W_ih_scales, b_ih, gh, out):
@@ -88,13 +89,13 @@ def tile_grucellmodel_pa_s_kernel(tc, input_seq, W_ih_words, W_ih_scales, b_ih, 
             return w_words[:, 2 * H * g : 2 * H * (g + 1)].bitcast(FP4X4), w_scales[:, H * g : H * (g + 1)]
 
         def transpose_gh():
-            ps = psum_t.tile([P, 2 * H], F32, tag="turn", name="gh_ps")
+            ps = psum_rz.tile([P, 2 * H], F32, tag="g_rz", name="gh_ps")
             nc.tensor.matmul(out=ps[:, 0:H], lhsT=gh_sb[:, 0:H], rhs=ident_bf[:], start=True, stop=True)
             nc.tensor.matmul(out=ps[:, H : 2 * H], lhsT=gh_sb[:, 2 * H : 3 * H], rhs=ident_bf[:], start=True, stop=True)
             nc.vector.tensor_copy(out=gh_t[:], in_=ps[:])
 
         def make_consts():
-            ps = psum_t.tile([P, H + 4], F32, tag="turn", name="consts_ps")
+            ps = psum_rz.tile([P, H + 4], F32, tag="g_rz", name="consts_ps")
             nc.tensor.matmul(out=ps[:, 0:H], lhsT=ident_bf[:], rhs=gh_sb[:, H : 2 * H], start=True, stop=False)
             nc.tensor.matmul(out=ps[:, 0:H], lhsT=ones[:], rhs=bias_rows[:, H : 2 * H], start=False, stop=True)
             nc.tensor.matmul(out=ps[:, H : H + 2], lhsT=bias_rows[:, 0:H], rhs=ones[:, 0:2], start=True, stop=True)
@@ -102,6 +103,7 @@ def tile_grucellmodel_pa_s_kernel(tc, input_seq, W_ih_words, W_ih_scales, b_ih, 
             nc.scalar.copy(out=consts[:], in_=ps[:])
 
         t = {}
+        z_group = {c: group for group in Z_GROUPS for c in group}
         n_banks = [psum_n.tile([P, BANK // B, B], F32, name="n_bank%d" % i) for i in range(3)]
         n_place = []
         for n in CHUNKS:
@@ -139,7 +141,7 @@ def tile_grucellmodel_pa_s_kernel(tc, input_seq, W_ih_words, W_ih_scales, b_ih, 
         def multiply(c):
             n = CHUNKS[c]
             x_codes, x_scales = t["codes", c], t["scales", c]
-            g_rz = psum_rz.tile([P, 2, n, B], F32, name="g_rz")
+            g_rz = psum_rz.tile([P, 2, n, B], F32, tag="g_rz", name="g_rz")
             t["g_r", c], t["g_z", c] = g_rz[:, 0, :, :], g_rz[:, 1, :, :]
             bank, slot = n_place[c]
             t["g_n", c] = n_banks[bank][:, slot : slot + n, :]
@@ -171,12 +173,21 @@ def tile_grucellmodel_pa_s_kernel(tc, input_seq, W_ih_words, W_ih_scales, b_ih, 
 
         def add_z_gate(c):
             n = CHUNKS[c]
-            t["pre_z", c] = gates.tile([P, n, H], F32, name="pre_z")
-            nc.vector.tensor_tensor(out=t["pre_z", c][:], in0=t["g_z", c], in1=over_steps(add_z, n), op=ALU.add)
+            group = z_group[c]
+            if c == group[0]:
+                steps = sum(CHUNKS[k] for k in group)
+                t["pre_z", group] = gates.tile([P, steps, H], F32, name="pre_z")
+                t["zc", group] = gates.tile([P, steps, H], F32, name="zc")
+            at = first[c] - first[group[0]]
+            t["zc", c] = t["zc", group][:, at : at + n, :]
+            nc.vector.tensor_tensor(
+                out=t["pre_z", group][:, at : at + n, :], in0=t["g_z", c], in1=over_steps(add_z, n), op=ALU.add
+            )
 
         def sigmoid_z(c):
-            t["zc", c] = gates.tile([P, CHUNKS[c], H], F32, name="zc")
-            nc.scalar.activation(out=t["zc", c][:], in_=t["pre_z", c][:], func=ACT.Sigmoid, scale=-1.0)
+            group = z_group[c]
+            if c == group[-1]:
+                nc.scalar.activation(out=t["zc", group][:], in_=t["pre_z", group][:], func=ACT.Sigmoid, scale=-1.0)
 
         def reset_hidden(c):
             n = CHUNKS[c]
@@ -200,7 +211,7 @@ def tile_grucellmodel_pa_s_kernel(tc, input_seq, W_ih_words, W_ih_scales, b_ih, 
         def new_state(c):
             n = CHUNKS[c]
             h_new = gates.tile([P, n, H], F32, name="h_new")
-            nc.vector.tensor_tensor(out=h_new[:], in0=t["n_ps", c][:], in1=t["zc", c][:], op=ALU.mult)
+            nc.vector.tensor_tensor(out=h_new[:], in0=t["n_ps", c][:], in1=t["zc", c], op=ALU.mult)
             nc.sync.dma_start(out=out[:, first[c] : first[c] + n, :], in_=h_new[:])
 
         chain = (

from contextlib import ExitStack

import concourse.mybir as mybir
from concourse.masks import make_identity

F32 = mybir.dt.float32
BF16 = mybir.dt.bfloat16
I32 = mybir.dt.int32
U32 = mybir.dt.uint32
U8 = mybir.dt.uint8
FP8X4 = mybir.dt.float8_e4m3fn_x4
FP4X4 = mybir.dt.float4_e2m1fn_x4
ACT = mybir.ActivationFunctionType
ALU = mybir.AluOpType

P = 128
T, B, K, H = 10, 128, 512, 128
GATES = 3 * H
PACK = 4
HALVES = 2
BANK = 512

FLOPS = 2 * T * B * K * GATES

CHUNKS = (1, 2, 2, 2, 2, 1)
Z_GROUPS = ((0,), (1, 2), (3, 4, 5))


def tile_grucellmodel_pa_s_kernel(tc, input_seq, W_ih_words, W_ih_scales, b_ih, gh, out):
    nc = tc.nc
    n_chunks = len(CHUNKS)
    first = [sum(CHUNKS[:c]) for c in range(n_chunks)]
    with ExitStack() as ctx:
        const = ctx.enter_context(tc.tile_pool(name="const", bufs=1))
        xin = ctx.enter_context(tc.tile_pool(name="xin", bufs=n_chunks))
        stage = ctx.enter_context(tc.tile_pool(name="stage", bufs=n_chunks))
        gates = ctx.enter_context(tc.tile_pool(name="gates", bufs=n_chunks))
        psum_t = ctx.enter_context(tc.psum_pool(name="psum_t", bufs=3))
        psum_rz = ctx.enter_context(tc.psum_pool(name="psum_rz", bufs=2))
        psum_n = ctx.enter_context(tc.psum_pool(name="psum_n", bufs=1))

        bias_rows = const.tile([P, GATES], BF16)
        ones = const.tile([P, P], BF16)
        warm = const.tile([P, 1], F32)
        ident = const.tile([P, P], F32)
        ident_bf = const.tile([P, P], BF16)
        gh_sb = const.tile([P, GATES], BF16)
        gh_t = const.tile([P, 2 * H], F32)
        consts = const.tile([P, H + 4], F32)
        w_words = const.tile([P, 2 * GATES], U8, align_bytes=64)
        w_scales = const.tile([P, GATES], U8, align_bytes=64)

        nc.vector.memset(bias_rows[:], 0.0)
        nc.vector.memset(w_scales[:].bitcast(I32), 0)
        nc.vector.memset(ones[:], 1.0)
        nc.vector.memset(warm[:], 0.0)

        x_tiles = {}

        def load_x(c):
            x_tiles[c] = xin.tile([P, CHUNKS[c], K], BF16, name="x_sb")
            steps = input_seq[first[c] : first[c] + CHUNKS[c]]
            nc.sync.dma_start(out=x_tiles[c][:], in_=steps.rearrange("t b k -> b t k"))

        make_identity(nc, ident[:])
        nc.scalar.dma_start(out=gh_sb[:], in_=gh)
        load_x(0)
        nc.sync.dma_start(out=bias_rows[0:1, :], in_=b_ih.unsqueeze(0))
        load_x(1)
        load_x(2)
        nc.sync.dma_start(out=w_words[:].bitcast(I32), in_=W_ih_words[0].bitcast(I32))
        load_x(3)
        scale_rows = W_ih_scales[0].bitcast(I32)
        for r in range(4):
            nc.sync.dma_start(out=w_scales[r:P:32, :].bitcast(I32), in_=scale_rows[r:16:4, :])
        for c in range(4, n_chunks):
            load_x(c)

        nc.scalar.activation(out=warm[:], in_=warm[:], func=ACT.Sigmoid)
        nc.vector.tensor_copy(out=ident_bf[:], in_=ident[:])

        gh_rT = gh_t[:, 0:H]
        gh_nT = gh_t[:, H : 2 * H]
        add_z = consts[:, 0:H]
        b_r = consts[:, H : H + 1]
        b_n = consts[:, H + 2 : H + 3]

        def w_gate(g):
            return w_words[:, 2 * H * g : 2 * H * (g + 1)].bitcast(FP4X4), w_scales[:, H * g : H * (g + 1)]

        def transpose_gh():
            ps = psum_rz.tile([P, 2 * H], F32, tag="g_rz", name="gh_ps")
            nc.tensor.matmul(out=ps[:, 0:H], lhsT=gh_sb[:, 0:H], rhs=ident_bf[:], start=True, stop=True)
            nc.tensor.matmul(out=ps[:, H : 2 * H], lhsT=gh_sb[:, 2 * H : 3 * H], rhs=ident_bf[:], start=True, stop=True)
            nc.vector.tensor_copy(out=gh_t[:], in_=ps[:])

        def make_consts():
            ps = psum_rz.tile([P, H + 4], F32, tag="g_rz", name="consts_ps")
            nc.tensor.matmul(out=ps[:, 0:H], lhsT=ident_bf[:], rhs=gh_sb[:, H : 2 * H], start=True, stop=False)
            nc.tensor.matmul(out=ps[:, 0:H], lhsT=ones[:], rhs=bias_rows[:, H : 2 * H], start=False, stop=True)
            nc.tensor.matmul(out=ps[:, H : H + 2], lhsT=bias_rows[:, 0:H], rhs=ones[:, 0:2], start=True, stop=True)
            nc.tensor.matmul(out=ps[:, H + 2 : H + 4], lhsT=bias_rows[:, 2 * H : 3 * H], rhs=ones[:, 0:2], start=True, stop=True)
            nc.scalar.copy(out=consts[:], in_=ps[:])

        t = {}
        z_group = {c: group for group in Z_GROUPS for c in group}
        n_banks = [psum_n.tile([P, BANK // B, B], F32, name="n_bank%d" % i) for i in range(3)]
        n_place = []
        for n in CHUNKS:
            bank, slot = n_place[-1] if n_place else (0, 0)
            slot += CHUNKS[len(n_place) - 1] if n_place else 0
            if slot + n > BANK // B:
                bank, slot = bank + 1, 0
            n_place.append((bank, slot))

        def over_steps(ap, n):
            return ap.unsqueeze(1).to_broadcast([P, n, P])

        def turn_x(c):
            n = CHUNKS[c]
            t["xt", c] = psum_t.tile([P, n, HALVES, B], F32, tag="turn", name="xt")
            for j in range(n):
                x_words = x_tiles[c][:, j, :].bitcast(F32)
                for u in range(HALVES):
                    nc.tensor.transpose(t["xt", c][:, j, u, :], x_words[:, u : K // 2 : HALVES], ident[:])

        def group_x(c):
            n = CHUNKS[c]
            t["grouped", c] = stage.tile([P, n * B * PACK], BF16, align_bytes=64, name="grouped")
            nc.scalar.copy(
                out=t["grouped", c][:].bitcast(F32).rearrange("p (j b u) -> p j b u", j=n, u=HALVES),
                in_=t["xt", c][:].rearrange("p j u b -> p j b u"),
            )

        def quantise_x(c):
            n = CHUNKS[c]
            t["codes", c] = stage.tile([P, n * B], U32, align_bytes=64, name="x_codes")
            t["scales", c] = stage.tile([P, n * B], U8, align_bytes=64, name="x_scales")
            nc.vector.quantize_mx(out=t["codes", c][:].bitcast(FP8X4), scales=t["scales", c][:], in_=t["grouped", c][:])

        def multiply(c):
            n = CHUNKS[c]
            x_codes, x_scales = t["codes", c], t["scales", c]
            g_rz = psum_rz.tile([P, 2, n, B], F32, tag="g_rz", name="g_rz")
            t["g_r", c], t["g_z", c] = g_rz[:, 0, :, :], g_rz[:, 1, :, :]
            bank, slot = n_place[c]
            t["g_n", c] = n_banks[bank][:, slot : slot + n, :]
            for dst, g in ((t["g_r", c], 0), (t["g_n", c], 2)):
                w, ws = w_gate(g)
                nc.tensor.matmul_mx(
                    out=dst.rearrange("p j b -> p (j b)"),
                    lhsT=w, lhsT_scale=ws,
                    rhs=x_codes[:].bitcast(FP8X4), rhs_scale=x_scales[:],
                    start=True, stop=True,
                )
            w, ws = w_gate(1)
            for j in range(n):
                nc.tensor.matmul_mx(
                    out=t["g_z", c][:, j, :],
                    lhsT=x_codes[:, j * B : (j + 1) * B].bitcast(FP8X4), lhsT_scale=x_scales[:, j * B : (j + 1) * B],
                    rhs=w, rhs_scale=ws,
                    start=True, stop=True,
                )

        def add_r(c):
            n = CHUNKS[c]
            t["pre_r", c] = gates.tile([P, n, B], F32, name="pre_r")
            nc.vector.tensor_tensor(out=t["pre_r", c][:], in0=t["g_r", c], in1=over_steps(gh_rT, n), op=ALU.add)

        def sigmoid_r(c):
            t["r", c] = gates.tile([P, CHUNKS[c], B], F32, name="r_t")
            nc.scalar.activation(out=t["r", c][:], in_=t["pre_r", c][:], func=ACT.Sigmoid, bias=b_r)

        def add_z_gate(c):
            n = CHUNKS[c]
            group = z_group[c]
            if c == group[0]:
                steps = sum(CHUNKS[k] for k in group)
                t["pre_z", group] = gates.tile([P, steps, H], F32, name="pre_z")
                t["zc", group] = gates.tile([P, steps, H], F32, name="zc")
            at = first[c] - first[group[0]]
            t["zc", c] = t["zc", group][:, at : at + n, :]
            nc.vector.tensor_tensor(
                out=t["pre_z", group][:, at : at + n, :], in0=t["g_z", c], in1=over_steps(add_z, n), op=ALU.add
            )

        def sigmoid_z(c):
            group = z_group[c]
            if c == group[-1]:
                nc.scalar.activation(out=t["zc", group][:], in_=t["pre_z", group][:], func=ACT.Sigmoid, scale=-1.0)

        def reset_hidden(c):
            n = CHUNKS[c]
            t["cand", c] = gates.tile([P, n, B], F32, name="cand")
            nc.gpsimd.tensor_tensor(out=t["cand", c][:], in0=t["r", c][:], in1=over_steps(gh_nT, n), op=ALU.mult)

        def add_n(c):
            t["pre_n", c] = gates.tile([P, CHUNKS[c], B], F32, name="pre_n")
            nc.vector.tensor_tensor(out=t["pre_n", c][:], in0=t["g_n", c], in1=t["cand", c][:], op=ALU.add)

        def tanh_n(c):
            t["n", c] = gates.tile([P, CHUNKS[c], B], F32, name="n_t")
            nc.scalar.activation(out=t["n", c][:], in_=t["pre_n", c][:], func=ACT.Tanh, bias=b_n)

        def turn_n(c):
            n = CHUNKS[c]
            t["n_ps", c] = psum_t.tile([P, n, H], F32, tag="turn", name="n_ps")
            for j in range(n):
                nc.tensor.transpose(t["n_ps", c][:, j, :], t["n", c][:, j, :], ident[:])

        def new_state(c):
            n = CHUNKS[c]
            h_new = gates.tile([P, n, H], F32, name="h_new")
            nc.vector.tensor_tensor(out=h_new[:], in0=t["n_ps", c][:], in1=t["zc", c], op=ALU.mult)
            nc.sync.dma_start(out=out[:, first[c] : first[c] + n, :], in_=h_new[:])

        chain = (
            (turn_x, 0), (group_x, 1), (quantise_x, 2), (multiply, 3), (add_z_gate, 4), (add_r, 4), (sigmoid_z, 5),
            (sigmoid_r, 5), (reset_hidden, 6), (add_n, 7), (tanh_n, 8), (turn_n, 9), (new_state, 10),
        )
        ctx.enter_context(tc.manual_schedule())
        warm_ps = psum_t.tile([P, BANK // P, P], F32, tag="turn", name="warm_ps")
        for j in range(8):
            nc.tensor.transpose(warm_ps[:, j % (BANK // P), :], ident[:], ident[:])
        for rnd in range(n_chunks + 10):
            if rnd == 3:
                turn_x(rnd)
            for work, lag in reversed(chain):
                if 0 <= rnd - lag < n_chunks and not (rnd == 3 and lag == 0):
                    work(rnd - lag)
            if rnd == 0:
                transpose_gh()
            if rnd == 2:
                make_consts()
